import numpy as np
import ml_dtypes

BF16 = ml_dtypes.bfloat16


def bf(x):
    return np.asarray(x, np.float32).astype(BF16)


def f32(x):
    return np.asarray(x, np.float32)


def f64(x):
    return np.asarray(x).astype(np.float64)


def striped(idx):
    return np.tile(idx.reshape(-1, 16).T, (8, 1))


D, V, M, B, T, N = 128, 4096, 128, 64, 128, 8192


def setup_inputs():
    return {"table": bf(np.random.standard_normal((D, V))), "w_emb": bf(0.5 * np.random.standard_normal((D, M))), "pos_tab": bf(np.random.standard_normal((D, T))), "w_pos": bf(0.5 * np.random.standard_normal((D, M))), "b": f32(0.1 * np.random.standard_normal((M, 1))), "offs": striped(np.random.permutation(np.tile(np.arange(V), 2))[:N])}


def reference(table, w_emb, pos_tab, w_pos, b, offs):
    idx = offs[:16].T.reshape(-1)
    y = f64(w_emb).T @ f64(table)[:, idx]
    q = f64(w_pos).T @ f64(pos_tab)
    tok = y.reshape(M, B, T) + q[:, None, :]
    return np.maximum(tok.sum(axis=2) / T + f64(b), 0.0)

@@ -1,0 +1,62 @@
+import concourse.mybir as mybir
+
+P = 128
+V = 4096
+N = 8192
+T = 128
+B = N // T
+PIECE = 512
+PIECES = N // PIECE
+SENTENCES = PIECE // T
+OFFSET_COLUMNS = PIECE // 16
+
+BF16, F32, U16 = mybir.dt.bfloat16, mybir.dt.float32, mybir.dt.uint16
+ADD, MULT = mybir.AluOpType.add, mybir.AluOpType.mult
+X = mybir.AxisListType.X
+RELU = mybir.ActivationFunctionType.Relu
+
+FLOPS = 2 * P * P * N + 2 * P * P * T
+
+
+def tile_dan_kernel(tc, table, w_emb, pos_tab, w_pos, b, offs, out):
+    nc = tc.nc
+    with (
+        tc.tile_pool(name="held", bufs=1) as held,
+        tc.psum_pool(name="position_bank", bufs=1) as position_bank,
+        tc.psum_pool(name="word_banks", bufs=7) as word_banks,
+    ):
+        offsets = held.tile([P, N // 16], U16, name="offsets")
+        nc.sync.dma_start(offsets[:], offs)
+        words = held.tile([P, V], BF16, name="words")
+        nc.sync.dma_start(words[:], table)
+        word_weights = held.tile([P, P], BF16, name="word_weights")
+        nc.scalar.dma_start(word_weights[:], w_emb)
+        position_weights = held.tile([P, P], BF16, name="position_weights")
+        nc.scalar.dma_start(position_weights[:], w_pos)
+        positions = held.tile([P, T], BF16, name="positions")
+        nc.scalar.dma_start(positions[:], pos_tab)
+        bias = held.tile([P, 1], F32, name="bias")
+        nc.scalar.dma_start(bias[:], b)
+
+        q = position_bank.tile([P, T], F32, name="q")
+        nc.tensor.matmul(q[:], position_weights[:], positions[:], start=True, stop=True)
+        q_sum = held.tile([P, 1], F32, name="q_sum")
+        nc.vector.tensor_reduce(q_sum[:], q[:], X, ADD)
+        shift = held.tile([P, 1], F32, name="shift")
+        nc.vector.tensor_scalar(shift[:], q_sum[:], 1.0 / T, bias[:, 0:1], MULT, ADD)
+
+        sums = held.tile([P, B], F32, name="sums")
+        for u in range(PIECES):
+            y = word_banks.tile([P, PIECE], F32, name="y")
+            picked = words[:].indirect(offsets[:, u * OFFSET_COLUMNS : (u + 1) * OFFSET_COLUMNS])
+            nc.tensor.matmul(y[:], word_weights[:], picked, start=True, stop=True)
+            nc.vector.tensor_reduce(
+                sums[:, u * SENTENCES : (u + 1) * SENTENCES],
+                y[:].rearrange("p (s t) -> p s t", t=T),
+                X,
+                ADD,
+            )
+
+        result = held.tile([P, B], F32, name="result")
+        nc.scalar.activation(result[:], sums[:], RELU, bias=shift[:, 0:1], scale=1.0 / T)
+        nc.sync.dma_start(out, result[:])

@@ -28,15 +28,15 @@ def tile_dan_kernel(tc, table, w_emb, pos_tab, w_pos, b, offs, out):
         offsets = held.tile([P, N // 16], U16, name="offsets")
         nc.sync.dma_start(offsets[:], offs)
         words = held.tile([P, V], BF16, name="words")
-        nc.sync.dma_start(words[:], table)
+        nc.scalar.dma_start(words[:], table)
         word_weights = held.tile([P, P], BF16, name="word_weights")
-        nc.scalar.dma_start(word_weights[:], w_emb)
+        nc.sync.dma_start(word_weights[:], w_emb)
         position_weights = held.tile([P, P], BF16, name="position_weights")
-        nc.scalar.dma_start(position_weights[:], w_pos)
+        nc.sync.dma_start(position_weights[:], w_pos)
         positions = held.tile([P, T], BF16, name="positions")
-        nc.scalar.dma_start(positions[:], pos_tab)
+        nc.sync.dma_start(positions[:], pos_tab)
         bias = held.tile([P, 1], F32, name="bias")
-        nc.scalar.dma_start(bias[:], b)
+        nc.sync.dma_start(bias[:], b)
 
         q = position_bank.tile([P, T], F32, name="q")
         nc.tensor.matmul(q[:], position_weights[:], positions[:], start=True, stop=True)

@@ -9,6 +9,7 @@ PIECE = 512
 PIECES = N // PIECE
 SENTENCES = PIECE // T
 OFFSET_COLUMNS = PIECE // 16
+LATE_SENTENCES = 8
 
 BF16, F32, U16 = mybir.dt.bfloat16, mybir.dt.float32, mybir.dt.uint16
 ADD, MULT = mybir.AluOpType.add, mybir.AluOpType.mult
@@ -46,7 +47,9 @@ def tile_dan_kernel(tc, table, w_emb, pos_tab, w_pos, b, offs, out):
         nc.vector.tensor_scalar(shift[:], q_sum[:], 1.0 / T, bias[:, 0:1], MULT, ADD)
 
         sums = held.tile([P, B], F32, name="sums")
-        for u in range(PIECES):
+        result = held.tile([P, B], F32, name="result")
+
+        def look_up_and_sum(u):
             y = word_banks.tile([P, PIECE], F32, name="y")
             picked = words[:].indirect(offsets[:, u * OFFSET_COLUMNS : (u + 1) * OFFSET_COLUMNS])
             nc.tensor.matmul(y[:], word_weights[:], picked, start=True, stop=True)
@@ -57,6 +60,16 @@ def tile_dan_kernel(tc, table, w_emb, pos_tab, w_pos, b, offs, out):
                 ADD,
             )
 
-        result = held.tile([P, B], F32, name="result")
-        nc.scalar.activation(result[:], sums[:], RELU, bias=shift[:, 0:1], scale=1.0 / T)
-        nc.sync.dma_start(out, result[:])
+        def finish(first, end):
+            nc.scalar.activation(
+                result[:, first:end], sums[:, first:end], RELU, bias=shift[:, 0:1], scale=1.0 / T
+            )
+            nc.sync.dma_start(out[:, first:end], result[:, first:end])
+
+        early_pieces = (B - LATE_SENTENCES) // SENTENCES
+        for u in range(early_pieces):
+            look_up_and_sum(u)
+        finish(0, B - LATE_SENTENCES)
+        for u in range(early_pieces, PIECES):
+            look_up_and_sum(u)
+        finish(B - LATE_SENTENCES, B)

@@ -9,7 +9,6 @@ PIECE = 512
 PIECES = N // PIECE
 SENTENCES = PIECE // T
 OFFSET_COLUMNS = PIECE // 16
-LATE_SENTENCES = 8
 
 BF16, F32, U16 = mybir.dt.bfloat16, mybir.dt.float32, mybir.dt.uint16
 ADD, MULT = mybir.AluOpType.add, mybir.AluOpType.mult
@@ -64,12 +63,10 @@ def tile_dan_kernel(tc, table, w_emb, pos_tab, w_pos, b, offs, out):
             nc.scalar.activation(
                 result[:, first:end], sums[:, first:end], RELU, bias=shift[:, 0:1], scale=1.0 / T
             )
-            nc.sync.dma_start(out[:, first:end], result[:, first:end])
 
-        early_pieces = (B - LATE_SENTENCES) // SENTENCES
-        for u in range(early_pieces):
+        for u in range(PIECES - 1):
             look_up_and_sum(u)
-        finish(0, B - LATE_SENTENCES)
-        for u in range(early_pieces, PIECES):
-            look_up_and_sum(u)
-        finish(B - LATE_SENTENCES, B)
+        finish(0, B - SENTENCES)
+        look_up_and_sum(PIECES - 1)
+        finish(B - SENTENCES, B)
+        nc.sync.dma_start(out, result[:])

@@ -11,9 +11,8 @@ SENTENCES = PIECE // T
 OFFSET_COLUMNS = PIECE // 16
 
 BF16, F32, U16 = mybir.dt.bfloat16, mybir.dt.float32, mybir.dt.uint16
-ADD, MULT = mybir.AluOpType.add, mybir.AluOpType.mult
+ADD, MAX, MULT = mybir.AluOpType.add, mybir.AluOpType.max, mybir.AluOpType.mult
 X = mybir.AxisListType.X
-RELU = mybir.ActivationFunctionType.Relu
 
 FLOPS = 2 * P * P * N + 2 * P * P * T
 
@@ -29,14 +28,17 @@ def tile_dan_kernel(tc, table, w_emb, pos_tab, w_pos, b, offs, out):
         nc.sync.dma_start(offsets[:], offs)
         words = held.tile([P, V], BF16, name="words")
         nc.scalar.dma_start(words[:], table)
-        word_weights = held.tile([P, P], BF16, name="word_weights")
-        nc.sync.dma_start(word_weights[:], w_emb)
+        loaded_weights = held.tile([P, P], BF16, name="loaded_weights")
+        nc.sync.dma_start(loaded_weights[:], w_emb)
         position_weights = held.tile([P, P], BF16, name="position_weights")
         nc.sync.dma_start(position_weights[:], w_pos)
         positions = held.tile([P, T], BF16, name="positions")
         nc.sync.dma_start(positions[:], pos_tab)
         bias = held.tile([P, 1], F32, name="bias")
         nc.sync.dma_start(bias[:], b)
+
+        word_weights = held.tile([P, P], BF16, name="word_weights")
+        nc.vector.tensor_scalar(word_weights[:], loaded_weights[:], 1.0 / T, None, MULT)
 
         q = position_bank.tile([P, T], F32, name="q")
         nc.tensor.matmul(q[:], position_weights[:], positions[:], start=True, stop=True)
@@ -60,8 +62,8 @@ def tile_dan_kernel(tc, table, w_emb, pos_tab, w_pos, b, offs, out):
             )
 
         def finish(first, end):
-            nc.scalar.activation(
-                result[:, first:end], sums[:, first:end], RELU, bias=shift[:, 0:1], scale=1.0 / T
+            nc.vector.tensor_scalar(
+                result[:, first:end], sums[:, first:end], shift[:, 0:1], 0.0, ADD, MAX
             )
 
         for u in range(PIECES - 1):

import concourse.mybir as mybir

P = 128
V = 4096
N = 8192
T = 128
B = N // T
PIECE = 512
PIECES = N // PIECE
SENTENCES = PIECE // T
OFFSET_COLUMNS = PIECE // 16

BF16, F32, U16 = mybir.dt.bfloat16, mybir.dt.float32, mybir.dt.uint16
ADD, MAX, MULT = mybir.AluOpType.add, mybir.AluOpType.max, mybir.AluOpType.mult
X = mybir.AxisListType.X

FLOPS = 2 * P * P * N + 2 * P * P * T


def tile_dan_kernel(tc, table, w_emb, pos_tab, w_pos, b, offs, out):
    nc = tc.nc
    with (
        tc.tile_pool(name="held", bufs=1) as held,
        tc.psum_pool(name="position_bank", bufs=1) as position_bank,
        tc.psum_pool(name="word_banks", bufs=7) as word_banks,
    ):
        offsets = held.tile([P, N // 16], U16, name="offsets")
        nc.sync.dma_start(offsets[:], offs)
        words = held.tile([P, V], BF16, name="words")
        nc.scalar.dma_start(words[:], table)
        loaded_weights = held.tile([P, P], BF16, name="loaded_weights")
        nc.sync.dma_start(loaded_weights[:], w_emb)
        position_weights = held.tile([P, P], BF16, name="position_weights")
        nc.sync.dma_start(position_weights[:], w_pos)
        positions = held.tile([P, T], BF16, name="positions")
        nc.sync.dma_start(positions[:], pos_tab)
        bias = held.tile([P, 1], F32, name="bias")
        nc.sync.dma_start(bias[:], b)

        word_weights = held.tile([P, P], BF16, name="word_weights")
        nc.vector.tensor_scalar(word_weights[:], loaded_weights[:], 1.0 / T, None, MULT)

        q = position_bank.tile([P, T], F32, name="q")
        nc.tensor.matmul(q[:], position_weights[:], positions[:], start=True, stop=True)
        q_sum = held.tile([P, 1], F32, name="q_sum")
        nc.vector.tensor_reduce(q_sum[:], q[:], X, ADD)
        shift = held.tile([P, 1], F32, name="shift")
        nc.vector.tensor_scalar(shift[:], q_sum[:], 1.0 / T, bias[:, 0:1], MULT, ADD)

        sums = held.tile([P, B], F32, name="sums")
        result = held.tile([P, B], F32, name="result")

        def look_up_and_sum(u):
            y = word_banks.tile([P, PIECE], F32, name="y")
            picked = words[:].indirect(offsets[:, u * OFFSET_COLUMNS : (u + 1) * OFFSET_COLUMNS])
            nc.tensor.matmul(y[:], word_weights[:], picked, start=True, stop=True)
            nc.vector.tensor_reduce(
                sums[:, u * SENTENCES : (u + 1) * SENTENCES],
                y[:].rearrange("p (s t) -> p s t", t=T),
                X,
                ADD,
            )

        def finish(first, end):
            nc.vector.tensor_scalar(
                result[:, first:end], sums[:, first:end], shift[:, 0:1], 0.0, ADD, MAX
            )

        for u in range(PIECES - 1):
            look_up_and_sum(u)
        finish(0, B - SENTENCES)
        look_up_and_sum(PIECES - 1)
        finish(B - SENTENCES, B)
        nc.sync.dma_start(out, result[:])
